import numpy as np
import ml_dtypes


def mxq(x, axis, fmt="e4m3"):
    dtype, down = {"e4m3": (ml_dtypes.float8_e4m3fn, 7), "e5m2": (ml_dtypes.float8_e5m2, 14)}[fmt]
    v = np.moveaxis(np.asarray(x, np.float32).astype(ml_dtypes.bfloat16).astype(np.float64), axis, -1)
    blocks = v.reshape(v.shape[:-1] + (-1, 32))
    amax = np.abs(blocks).max(-1, keepdims=True)
    byte = np.maximum(np.where(amax > 0, np.frexp(amax)[1] - 1 + 127, 0) - down, 1)
    scale = np.exp2(byte - 127.0)
    codes = (blocks / scale).astype(np.float32).astype(dtype).astype(np.float64)
    return np.moveaxis((codes * scale).reshape(v.shape), -1, axis)


WIDE = False


def mx_kscale(k):
    if not WIDE:
        return np.ones(k)
    levels = np.array([10, -10, 5, -5, 0])
    a = np.random.permutation(np.resize(levels, k // 512 * 4)).reshape(k // 512, 4)
    idx = np.arange(k)
    return np.exp2(a[idx // 512, idx % 128 // 32])


BF16 = ml_dtypes.bfloat16


def bf(x):
    return np.asarray(x, np.float32).astype(BF16)


def f64(x):
    return np.asarray(x).astype(np.float64)


B, N0, N1, N2, N3, T, K = 256, 512, 1024, 1024, 512, 8, 512
R = min(K, N0, N1)
R2 = min(R, T)
GS = 0.25


def setup_inputs():
    s, t = mx_kscale(R), mx_kscale(R)
    return {"S": bf(np.random.standard_normal((R, R, R2)) * s[:, None, None] * t[None, :, None]),
            "U0": bf(np.random.standard_normal((N1, R)) / np.sqrt(R) / s[None, :]),
            "U1": bf(np.random.standard_normal((N0, R)) * GS / np.sqrt(R) / t[None, :])}


def reference(S, U0, U1):
    w1 = mxq(f64(S).reshape(R, R * R2).T, 1, "e4m3") @ mxq(f64(U0).T, 0, "e4m3")
    w2 = mxq(w1.reshape(R, R2 * N1).T, 1, "e4m3") @ mxq(f64(U1).T, 0, "e4m3")
    return w2.reshape(R2, N1, N0)

@@ -1,0 +1,193 @@
+from contextlib import ExitStack
+
+import concourse.mybir as mybir
+from concourse.masks import make_identity
+
+BF16 = mybir.dt.bfloat16
+F32 = mybir.dt.float32
+U32 = mybir.dt.uint32
+U8 = mybir.dt.uint8
+FP8X4 = mybir.dt.float8_e4m3fn_x4
+
+P = 128
+PACK = 4
+K = P * PACK
+R = 8
+J = 1024
+I = 512
+J_BLOCKS = J // P
+FACTOR_BLOCKS = 4
+R_HALF = R // 2
+UNIT = 4
+STORE_BANKS = 2
+BANKS = R * J_BLOCKS
+LAG = 6
+SCALAR_SHARE = 5
+
+FLOPS = 2 * K * (K * R) * J + 2 * K * (R * J) * I
+
+
+def quantise_factor(nc, psum, stage, identity, rows, codes, scales, tag):
+    grouped = stage.tile([P, FACTOR_BLOCKS, P, PACK], BF16, align_bytes=64, name="grouped")
+    for b in range(FACTOR_BLOCKS):
+        flipped = psum.tile([P, PACK, P], BF16, name="flipped", tag=tag)
+        for t in range(PACK):
+            nc.tensor.transpose(flipped[:, t, :], rows[:, b, t * P : (t + 1) * P], identity)
+        source = flipped[:].rearrange("x t a -> x a t")
+        if b % 2 == 0:
+            nc.vector.tensor_copy(out=grouped[:, b], in_=source)
+        else:
+            nc.scalar.copy(out=grouped[:, b], in_=source)
+    nc.vector.quantize_mx(
+        out=codes.bitcast(FP8X4),
+        scales=scales,
+        in_=grouped[:].rearrange("x b a t -> x (b a t)"),
+    )
+
+
+def tile_mtl_net_tf_pa_kernel(tc, S, U0, U1, out):
+    nc = tc.nc
+    with ExitStack() as ctx:
+        keep = ctx.enter_context(tc.tile_pool(name="keep", bufs=1))
+        stage = ctx.enter_context(tc.tile_pool(name="stage", bufs=3))
+        psum = ctx.enter_context(tc.psum_pool(name="psum", bufs=4))
+        ctx.enter_context(tc.manual_schedule())
+
+        u0_view = U0.rearrange("(a b) q -> a b q", b=J_BLOCKS)
+        u0_rows = keep.tile([P, J_BLOCKS, K], BF16)
+        for first in range(0, J_BLOCKS, FACTOR_BLOCKS):
+            blocks = slice(first, first + FACTOR_BLOCKS)
+            nc.sync.dma_start(out=u0_rows[:, blocks, :], in_=u0_view[:, blocks, :])
+        s_view = S.rearrange("(t x) p r -> x t p r", t=PACK)
+        s_raw = []
+        for c in range(PACK):
+            raw = keep.tile([P, PACK, P, R], BF16, name="s_raw%d" % c)
+            nc.sync.dma_start(out=raw[:], in_=s_view[:, :, c * P : (c + 1) * P, :])
+            s_raw.append(raw)
+        u1_rows = keep.tile([P, FACTOR_BLOCKS, K], BF16)
+        nc.sync.dma_start(out=u1_rows[:], in_=U1.rearrange("(b a) p -> a b p", a=P))
+
+        identity = keep.tile([P, P], BF16)
+        make_identity(nc, identity[:])
+
+        u0_codes = keep.tile([P, J], U32, align_bytes=64)
+        u0_scales = keep.tile([P, J], U8, align_bytes=64)
+        for first in range(0, J_BLOCKS, FACTOR_BLOCKS):
+            columns = slice(first * P, (first + FACTOR_BLOCKS) * P)
+            quantise_factor(
+                nc,
+                psum,
+                stage,
+                identity[:],
+                u0_rows[:, first : first + FACTOR_BLOCKS, :],
+                u0_codes[:, columns],
+                u0_scales[:, columns],
+                "one",
+            )
+
+        s_codes = keep.tile([P, 2, PACK, R_HALF * P], U32, align_bytes=64)
+        s_scales = keep.tile([P, 2, PACK, R_HALF * P], U8, align_bytes=64)
+        s_grouped = {}
+
+        def quantise_s(half, c):
+            nc.vector.quantize_mx(
+                out=s_codes[:, half, c, :].bitcast(FP8X4),
+                scales=s_scales[:, half, c, :],
+                in_=s_grouped[half, c][:].rearrange("x r y t -> x (r y t)"),
+            )
+
+        for c in range(PACK):
+            for half in range(2):
+                s_grouped[half, c] = keep.tile(
+                    [P, R_HALF, P, PACK], BF16, align_bytes=64, name="s_grouped%d%d" % (half, c)
+                )
+                target = s_grouped[half, c][:].rearrange("x r y t -> x y t r")
+                source = s_raw[c][:, :, :, half * R_HALF : (half + 1) * R_HALF].rearrange(
+                    "x t y r -> x y t r"
+                )
+                if half == 0:
+                    nc.vector.tensor_copy(out=target, in_=source)
+                else:
+                    nc.scalar.copy(out=target, in_=source)
+            quantise_s(0, c)
+
+        out_view = out.rearrange("r (a b) i -> r a b i", b=J_BLOCKS)
+        u1_codes = keep.tile([P, I], U32, align_bytes=64)
+        u1_scales = keep.tile([P, I], U8, align_bytes=64)
+        w1_grouped = {}
+        w1_codes = {}
+        w1_scales = {}
+        result = {}
+
+        def first_contraction(n):
+            r, b = divmod(n, J_BLOCKS)
+            half, r_low = divmod(r, R_HALF)
+            unit, place = divmod(n, UNIT)
+            if place == 0:
+                w1_grouped[unit] = stage.tile(
+                    [P, UNIT, P, PACK], BF16, align_bytes=64, name="w1_grouped"
+                )
+            w1_bank = psum.tile([P, PACK, P], F32, name="w1_bank", tag="one")
+            for c in range(PACK):
+                nc.tensor.matmul_mx(
+                    out=w1_bank[:, c, :],
+                    lhsT=s_codes[:, half, c, r_low * P : (r_low + 1) * P].bitcast(FP8X4),
+                    lhsT_scale=s_scales[:, half, c, r_low * P : (r_low + 1) * P],
+                    rhs=u0_codes[:, b * P : (b + 1) * P].bitcast(FP8X4),
+                    rhs_scale=u0_scales[:, b * P : (b + 1) * P],
+                    start=True,
+                    stop=True,
+                )
+            source = w1_bank[:].rearrange("y c a -> y a c")
+            if n % SCALAR_SHARE == SCALAR_SHARE - 1 or (n < LAG and n % 2 == 1):
+                nc.scalar.copy(out=w1_grouped[unit][:, place], in_=source)
+            else:
+                nc.vector.tensor_copy(out=w1_grouped[unit][:, place], in_=source)
+
+        def quantise_w1(unit):
+            w1_codes[unit] = stage.tile([P, UNIT * P], U32, align_bytes=64, name="w1_codes")
+            w1_scales[unit] = stage.tile([P, UNIT * P], U8, align_bytes=64, name="w1_scales")
+            nc.vector.quantize_mx(
+                out=w1_codes[unit][:].bitcast(FP8X4),
+                scales=w1_scales[unit][:],
+                in_=w1_grouped[unit][:].rearrange("y u a c -> y (u a c)"),
+            )
+
+        def second_contraction(n):
+            r, b = divmod(n, J_BLOCKS)
+            unit, place = divmod(n, UNIT)
+            batch, slot = divmod(n, STORE_BANKS)
+            if slot == 0:
+                result[batch] = stage.tile([P, STORE_BANKS, I], F32, name="result", bufs=4)
+            out_bank = psum.tile([P, I], F32, name="out_bank", tag="two")
+            nc.tensor.matmul_mx(
+                out=out_bank[:],
+                lhsT=w1_codes[unit][:, place * P : (place + 1) * P].bitcast(FP8X4),
+                lhsT_scale=w1_scales[unit][:, place * P : (place + 1) * P],
+                rhs=u1_codes[:].bitcast(FP8X4),
+                rhs_scale=u1_scales[:],
+                start=True,
+                stop=True,
+            )
+            if n >= BANKS - LAG and n % 2 == 1:
+                nc.vector.tensor_copy(out=result[batch][:, slot, :], in_=out_bank[:])
+            else:
+                nc.scalar.copy(out=result[batch][:, slot, :], in_=out_bank[:])
+            if slot == STORE_BANKS - 1:
+                nc.sync.dma_start(out=out_view[r, :, b - slot : b + 1, :], in_=result[batch][:])
+
+        def step(n):
+            if n < BANKS:
+                first_contraction(n)
+            if n % UNIT == 0 and UNIT <= n <= BANKS:
+                quantise_w1(n // UNIT - 1)
+            if n % UNIT == 2 and n // UNIT < PACK:
+                quantise_s(1, n // UNIT)
+            if n >= LAG:
+                second_contraction(n - LAG)
+
+        for n in range(LAG):
+            step(n)
+        quantise_factor(nc, psum, stage, identity[:], u1_rows, u1_codes[:], u1_scales[:], "two")
+        for n in range(LAG, BANKS + LAG):
+            step(n)

@@ -21,19 +21,36 @@ R_HALF = R // 2
 UNIT = 4
 STORE_BANKS = 2
 BANKS = R * J_BLOCKS
-LAG = 6
+LAG = 8
 SCALAR_SHARE = 5
 
 FLOPS = 2 * K * (K * R) * J + 2 * K * (R * J) * I
 
 
-def quantise_factor(nc, psum, stage, identity, rows, codes, scales, tag):
-    grouped = stage.tile([P, FACTOR_BLOCKS, P, PACK], BF16, align_bytes=64, name="grouped")
+def quantise_u0_blocks(nc, psum, stage, identity, rows, codes, scales):
+    grouped = stage.tile([P, FACTOR_BLOCKS * P * PACK], BF16, align_bytes=64, name="u0_grouped")
+    grouped_words = grouped[:].bitcast(F32).rearrange("x (b a u) -> x b a u", b=FACTOR_BLOCKS, u=2)
+    for first in range(0, FACTOR_BLOCKS, 2):
+        flipped = psum.tile([P, 2, 2, P], F32, name="u0_flipped", tag="one")
+        for b in range(2):
+            words = rows[:, first + b, :].bitcast(F32)
+            for u in range(2):
+                nc.tensor.transpose(flipped[:, b, u, :], words[:, u * P : (u + 1) * P], identity)
+        source = flipped[:].rearrange("x b u a -> x b a u")
+        if first == 0:
+            nc.vector.tensor_copy(out=grouped_words[:, first : first + 2], in_=source)
+        else:
+            nc.scalar.copy(out=grouped_words[:, first : first + 2], in_=source)
+    nc.vector.quantize_mx(out=codes.bitcast(FP8X4), scales=scales, in_=grouped[:])
+
+
+def quantise_u1(nc, psum, stage, identity, rows, codes, scales):
+    grouped = stage.tile([P, FACTOR_BLOCKS, P, PACK], BF16, align_bytes=64, name="u1_grouped")
     for b in range(FACTOR_BLOCKS):
-        flipped = psum.tile([P, PACK, P], BF16, name="flipped", tag=tag)
+        flipped = psum.tile([P, PACK, P], BF16, name="u1_flipped", tag="two")
         for t in range(PACK):
             nc.tensor.transpose(flipped[:, t, :], rows[:, b, t * P : (t + 1) * P], identity)
-        source = flipped[:].rearrange("x t a -> x a t")
+        source = flipped[:].rearrange("y t a -> y a t")
         if b % 2 == 0:
             nc.vector.tensor_copy(out=grouped[:, b], in_=source)
         else:
@@ -41,7 +58,7 @@ def quantise_factor(nc, psum, stage, identity, rows, codes, scales, tag):
     nc.vector.quantize_mx(
         out=codes.bitcast(FP8X4),
         scales=scales,
-        in_=grouped[:].rearrange("x b a t -> x (b a t)"),
+        in_=grouped[:].rearrange("y b a t -> y (b a t)"),
     )
 
 
@@ -58,15 +75,20 @@ def tile_mtl_net_tf_pa_kernel(tc, S, U0, U1, out):
         for first in range(0, J_BLOCKS, FACTOR_BLOCKS):
             blocks = slice(first, first + FACTOR_BLOCKS)
             nc.sync.dma_start(out=u0_rows[:, blocks, :], in_=u0_view[:, blocks, :])
-        s_view = S.rearrange("(t x) p r -> x t p r", t=PACK)
+        s_view = S.rearrange("(u x e) p r -> x u e p r", u=2, e=2)
         s_raw = []
         for c in range(PACK):
             raw = keep.tile([P, PACK, P, R], BF16, name="s_raw%d" % c)
-            nc.sync.dma_start(out=raw[:], in_=s_view[:, :, c * P : (c + 1) * P, :])
+            for u in range(2):
+                nc.sync.dma_start(
+                    out=raw[:, 2 * u : 2 * u + 2, :, :], in_=s_view[:, u, :, c * P : (c + 1) * P, :]
+                )
             s_raw.append(raw)
         u1_rows = keep.tile([P, FACTOR_BLOCKS, K], BF16)
         nc.sync.dma_start(out=u1_rows[:], in_=U1.rearrange("(b a) p -> a b p", a=P))
 
+        identity_words = keep.tile([P, P], F32)
+        make_identity(nc, identity_words[:])
         identity = keep.tile([P, P], BF16)
         make_identity(nc, identity[:])
 
@@ -74,20 +96,35 @@ def tile_mtl_net_tf_pa_kernel(tc, S, U0, U1, out):
         u0_scales = keep.tile([P, J], U8, align_bytes=64)
         for first in range(0, J_BLOCKS, FACTOR_BLOCKS):
             columns = slice(first * P, (first + FACTOR_BLOCKS) * P)
-            quantise_factor(
+            quantise_u0_blocks(
                 nc,
                 psum,
                 stage,
-                identity[:],
+                identity_words[:],
                 u0_rows[:, first : first + FACTOR_BLOCKS, :],
                 u0_codes[:, columns],
                 u0_scales[:, columns],
-                "one",
             )
 
         s_codes = keep.tile([P, 2, PACK, R_HALF * P], U32, align_bytes=64)
         s_scales = keep.tile([P, 2, PACK, R_HALF * P], U8, align_bytes=64)
         s_grouped = {}
+        w1_bank = {}
+
+        def w1_pass(n, c):
+            r, b = divmod(n, J_BLOCKS)
+            half, r_low = divmod(r, R_HALF)
+            if c == 0:
+                w1_bank[n] = psum.tile([P, PACK, P], F32, name="w1_bank", tag="one")
+            nc.tensor.matmul_mx(
+                out=w1_bank[n][:, c, :],
+                lhsT=s_codes[:, half, c, r_low * P : (r_low + 1) * P].bitcast(FP8X4),
+                lhsT_scale=s_scales[:, half, c, r_low * P : (r_low + 1) * P],
+                rhs=u0_codes[:, b * P : (b + 1) * P].bitcast(FP8X4),
+                rhs_scale=u0_scales[:, b * P : (b + 1) * P],
+                start=True,
+                stop=True,
+            )
 
         def quantise_s(half, c):
             nc.vector.quantize_mx(
@@ -110,6 +147,8 @@ def tile_mtl_net_tf_pa_kernel(tc, S, U0, U1, out):
                 else:
                     nc.scalar.copy(out=target, in_=source)
             quantise_s(0, c)
+            for n in range(UNIT):
+                w1_pass(n, c)
 
         out_view = out.rearrange("r (a b) i -> r a b i", b=J_BLOCKS)
         u1_codes = keep.tile([P, I], U32, align_bytes=64)
@@ -119,26 +158,13 @@ def tile_mtl_net_tf_pa_kernel(tc, S, U0, U1, out):
         w1_scales = {}
         result = {}
 
-        def first_contraction(n):
-            r, b = divmod(n, J_BLOCKS)
-            half, r_low = divmod(r, R_HALF)
+        def round_w1(n):
             unit, place = divmod(n, UNIT)
             if place == 0:
                 w1_grouped[unit] = stage.tile(
                     [P, UNIT, P, PACK], BF16, align_bytes=64, name="w1_grouped"
                 )
-            w1_bank = psum.tile([P, PACK, P], F32, name="w1_bank", tag="one")
-            for c in range(PACK):
-                nc.tensor.matmul_mx(
-                    out=w1_bank[:, c, :],
-                    lhsT=s_codes[:, half, c, r_low * P : (r_low + 1) * P].bitcast(FP8X4),
-                    lhsT_scale=s_scales[:, half, c, r_low * P : (r_low + 1) * P],
-                    rhs=u0_codes[:, b * P : (b + 1) * P].bitcast(FP8X4),
-                    rhs_scale=u0_scales[:, b * P : (b + 1) * P],
-                    start=True,
-                    stop=True,
-                )
-            source = w1_bank[:].rearrange("y c a -> y a c")
+            source = w1_bank[n][:].rearrange("y c a -> y a c")
             if n % SCALAR_SHARE == SCALAR_SHARE - 1 or (n < LAG and n % 2 == 1):
                 nc.scalar.copy(out=w1_grouped[unit][:, place], in_=source)
             else:
@@ -177,8 +203,11 @@ def tile_mtl_net_tf_pa_kernel(tc, S, U0, U1, out):
                 nc.sync.dma_start(out=out_view[r, :, b - slot : b + 1, :], in_=result[batch][:])
 
         def step(n):
+            if UNIT <= n < BANKS:
+                for c in range(PACK):
+                    w1_pass(n, c)
             if n < BANKS:
-                first_contraction(n)
+                round_w1(n)
             if n % UNIT == 0 and UNIT <= n <= BANKS:
                 quantise_w1(n // UNIT - 1)
             if n % UNIT == 2 and n // UNIT < PACK:
@@ -186,8 +215,8 @@ def tile_mtl_net_tf_pa_kernel(tc, S, U0, U1, out):
             if n >= LAG:
                 second_contraction(n - LAG)
 
-        for n in range(LAG):
+        for n in range(UNIT):
             step(n)
-        quantise_factor(nc, psum, stage, identity[:], u1_rows, u1_codes[:], u1_scales[:], "two")
-        for n in range(LAG, BANKS + LAG):
+        quantise_u1(nc, psum, stage, identity[:], u1_rows, u1_codes[:], u1_scales[:])
+        for n in range(UNIT, BANKS + LAG):
             step(n)

@@ -20,6 +20,7 @@ FACTOR_BLOCKS = 4
 R_HALF = R // 2
 UNIT = 4
 STORE_BANKS = 2
+STORES_IN_FLIGHT = 8
 BANKS = R * J_BLOCKS
 LAG = 8
 SCALAR_SHARE = 5
@@ -184,7 +185,9 @@ def tile_mtl_net_tf_pa_kernel(tc, S, U0, U1, out):
             unit, place = divmod(n, UNIT)
             batch, slot = divmod(n, STORE_BANKS)
             if slot == 0:
-                result[batch] = stage.tile([P, STORE_BANKS, I], F32, name="result", bufs=4)
+                result[batch] = stage.tile(
+                    [P, STORE_BANKS, I], F32, name="result", bufs=STORES_IN_FLIGHT
+                )
             out_bank = psum.tile([P, I], F32, name="out_bank", tag="two")
             nc.tensor.matmul_mx(
                 out=out_bank[:],

@@ -22,10 +22,17 @@ UNIT = 4
 STORE_BANKS = 2
 STORES_IN_FLIGHT = 8
 BANKS = R * J_BLOCKS
-LAG = 8
-SCALAR_SHARE = 5
+PSUM_BANKS = 8
+LAG = PSUM_BANKS
+SCALAR_SHARE = 8
 
 FLOPS = 2 * K * (K * R) * J + 2 * K * (R * J) * I
+
+
+def bank_indices(n):
+    j_half, rest = divmod(n, BANKS // 2)
+    r, place = divmod(rest, FACTOR_BLOCKS)
+    return r, j_half * FACTOR_BLOCKS + place
 
 
 def quantise_u0_blocks(nc, psum, stage, identity, rows, codes, scales):
@@ -68,14 +75,13 @@ def tile_mtl_net_tf_pa_kernel(tc, S, U0, U1, out):
     with ExitStack() as ctx:
         keep = ctx.enter_context(tc.tile_pool(name="keep", bufs=1))
         stage = ctx.enter_context(tc.tile_pool(name="stage", bufs=3))
-        psum = ctx.enter_context(tc.psum_pool(name="psum", bufs=4))
-        ctx.enter_context(tc.manual_schedule())
+        psum = ctx.enter_context(tc.psum_pool(name="psum", bufs=PSUM_BANKS // 2))
 
         u0_view = U0.rearrange("(a b) q -> a b q", b=J_BLOCKS)
         u0_rows = keep.tile([P, J_BLOCKS, K], BF16)
-        for first in range(0, J_BLOCKS, FACTOR_BLOCKS):
-            blocks = slice(first, first + FACTOR_BLOCKS)
-            nc.sync.dma_start(out=u0_rows[:, blocks, :], in_=u0_view[:, blocks, :])
+        first_half = slice(0, FACTOR_BLOCKS)
+        second_half = slice(FACTOR_BLOCKS, J_BLOCKS)
+        u1_rows = keep.tile([P, FACTOR_BLOCKS, K], BF16)
         s_view = S.rearrange("(u x e) p r -> x u e p r", u=2, e=2)
         s_raw = []
         for c in range(PACK):
@@ -85,56 +91,42 @@ def tile_mtl_net_tf_pa_kernel(tc, S, U0, U1, out):
                     out=raw[:, 2 * u : 2 * u + 2, :, :], in_=s_view[:, u, :, c * P : (c + 1) * P, :]
                 )
             s_raw.append(raw)
-        u1_rows = keep.tile([P, FACTOR_BLOCKS, K], BF16)
-        nc.sync.dma_start(out=u1_rows[:], in_=U1.rearrange("(b a) p -> a b p", a=P))
+            if c == 0:
+                nc.sync.dma_start(out=u0_rows[:, first_half, :], in_=u0_view[:, first_half, :])
+                nc.sync.dma_start(out=u1_rows[:], in_=U1.rearrange("(b a) p -> a b p", a=P))
+        nc.sync.dma_start(out=u0_rows[:, second_half, :], in_=u0_view[:, second_half, :])
 
         identity_words = keep.tile([P, P], F32)
         make_identity(nc, identity_words[:])
         identity = keep.tile([P, P], BF16)
         make_identity(nc, identity[:])
 
-        u0_codes = keep.tile([P, J], U32, align_bytes=64)
-        u0_scales = keep.tile([P, J], U8, align_bytes=64)
-        for first in range(0, J_BLOCKS, FACTOR_BLOCKS):
-            columns = slice(first * P, (first + FACTOR_BLOCKS) * P)
+        u0_codes = keep.tile([P, J_BLOCKS, P], U32, align_bytes=64)
+        u0_scales = keep.tile([P, J_BLOCKS, P], U8, align_bytes=64)
+        u1_codes = keep.tile([P, I], U32, align_bytes=64)
+        u1_scales = keep.tile([P, I], U8, align_bytes=64)
+        s_codes = keep.tile([P, 2, PACK, R_HALF * P], U32, align_bytes=64)
+        s_scales = keep.tile([P, 2, PACK, R_HALF * P], U8, align_bytes=64)
+        s_grouped = {}
+        w1_bank = {}
+        w1_grouped = {}
+        w1_codes = {}
+        w1_scales = {}
+        result = {}
+        out_view = out.rearrange("r (a b) i -> r a b i", b=J_BLOCKS)
+
+        def quantise_u0_half(blocks):
             quantise_u0_blocks(
                 nc,
                 psum,
                 stage,
                 identity_words[:],
-                u0_rows[:, first : first + FACTOR_BLOCKS, :],
-                u0_codes[:, columns],
-                u0_scales[:, columns],
+                u0_rows[:, blocks, :],
+                u0_codes[:, blocks, :].rearrange("x b a -> x (b a)"),
+                u0_scales[:, blocks, :].rearrange("x b a -> x (b a)"),
             )
 
-        s_codes = keep.tile([P, 2, PACK, R_HALF * P], U32, align_bytes=64)
-        s_scales = keep.tile([P, 2, PACK, R_HALF * P], U8, align_bytes=64)
-        s_grouped = {}
-        w1_bank = {}
-
-        def w1_pass(n, c):
-            r, b = divmod(n, J_BLOCKS)
-            half, r_low = divmod(r, R_HALF)
-            if c == 0:
-                w1_bank[n] = psum.tile([P, PACK, P], F32, name="w1_bank", tag="one")
-            nc.tensor.matmul_mx(
-                out=w1_bank[n][:, c, :],
-                lhsT=s_codes[:, half, c, r_low * P : (r_low + 1) * P].bitcast(FP8X4),
-                lhsT_scale=s_scales[:, half, c, r_low * P : (r_low + 1) * P],
-                rhs=u0_codes[:, b * P : (b + 1) * P].bitcast(FP8X4),
-                rhs_scale=u0_scales[:, b * P : (b + 1) * P],
-                start=True,
-                stop=True,
-            )
-
-        def quantise_s(half, c):
-            nc.vector.quantize_mx(
-                out=s_codes[:, half, c, :].bitcast(FP8X4),
-                scales=s_scales[:, half, c, :],
-                in_=s_grouped[half, c][:].rearrange("x r y t -> x (r y t)"),
-            )
-
-        for c in range(PACK):
+        def regroup_s(c):
             for half in range(2):
                 s_grouped[half, c] = keep.tile(
                     [P, R_HALF, P, PACK], BF16, align_bytes=64, name="s_grouped%d%d" % (half, c)
@@ -147,17 +139,31 @@ def tile_mtl_net_tf_pa_kernel(tc, S, U0, U1, out):
                     nc.vector.tensor_copy(out=target, in_=source)
                 else:
                     nc.scalar.copy(out=target, in_=source)
-            quantise_s(0, c)
-            for n in range(UNIT):
-                w1_pass(n, c)
 
-        out_view = out.rearrange("r (a b) i -> r a b i", b=J_BLOCKS)
-        u1_codes = keep.tile([P, I], U32, align_bytes=64)
-        u1_scales = keep.tile([P, I], U8, align_bytes=64)
-        w1_grouped = {}
-        w1_codes = {}
-        w1_scales = {}
-        result = {}
+        def quantise_s(half, c):
+            nc.vector.quantize_mx(
+                out=s_codes[:, half, c, :].bitcast(FP8X4),
+                scales=s_scales[:, half, c, :],
+                in_=s_grouped[half, c][:].rearrange("x r y t -> x (r y t)"),
+            )
+
+        def w1_pass(n, c):
+            r, b = bank_indices(n)
+            half, r_low = divmod(r, R_HALF)
+            if c == 0:
+                early_second_tag = PSUM_BANKS // 2 <= n < PSUM_BANKS
+                w1_bank[n] = psum.tile(
+                    [P, PACK, P], F32, name="w1_bank", tag="two" if early_second_tag else "one"
+                )
+            nc.tensor.matmul_mx(
+                out=w1_bank[n][:, c, :],
+                lhsT=s_codes[:, half, c, r_low * P : (r_low + 1) * P].bitcast(FP8X4),
+                lhsT_scale=s_scales[:, half, c, r_low * P : (r_low + 1) * P],
+                rhs=u0_codes[:, b, :].bitcast(FP8X4),
+                rhs_scale=u0_scales[:, b, :],
+                start=True,
+                stop=True,
+            )
 
         def round_w1(n):
             unit, place = divmod(n, UNIT)
@@ -166,7 +172,7 @@ def tile_mtl_net_tf_pa_kernel(tc, S, U0, U1, out):
                     [P, UNIT, P, PACK], BF16, align_bytes=64, name="w1_grouped"
                 )
             source = w1_bank[n][:].rearrange("y c a -> y a c")
-            if n % SCALAR_SHARE == SCALAR_SHARE - 1 or (n < LAG and n % 2 == 1):
+            if n % SCALAR_SHARE == SCALAR_SHARE - 1 or (n < LAG and n % UNIT != 0):
                 nc.scalar.copy(out=w1_grouped[unit][:, place], in_=source)
             else:
                 nc.vector.tensor_copy(out=w1_grouped[unit][:, place], in_=source)
@@ -181,7 +187,7 @@ def tile_mtl_net_tf_pa_kernel(tc, S, U0, U1, out):
             )
 
         def second_contraction(n):
-            r, b = divmod(n, J_BLOCKS)
+            r, b = bank_indices(n)
             unit, place = divmod(n, UNIT)
             batch, slot = divmod(n, STORE_BANKS)
             if slot == 0:
@@ -206,20 +212,29 @@ def tile_mtl_net_tf_pa_kernel(tc, S, U0, U1, out):
                 nc.sync.dma_start(out=out_view[r, :, b - slot : b + 1, :], in_=result[batch][:])
 
         def step(n):
-            if UNIT <= n < BANKS:
+            if PSUM_BANKS <= n < BANKS:
                 for c in range(PACK):
                     w1_pass(n, c)
             if n < BANKS:
                 round_w1(n)
             if n % UNIT == 0 and UNIT <= n <= BANKS:
                 quantise_w1(n // UNIT - 1)
-            if n % UNIT == 2 and n // UNIT < PACK:
-                quantise_s(1, n // UNIT)
+            if n % 2 == 1 and n // 2 < PACK:
+                quantise_s(1, n // 2)
             if n >= LAG:
                 second_contraction(n - LAG)
 
-        for n in range(UNIT):
+        for c in range(PACK):
+            regroup_s(c)
+            quantise_s(0, c)
+            if c == 0:
+                quantise_u0_half(first_half)
+                quantise_u1(nc, psum, stage, identity[:], u1_rows, u1_codes[:], u1_scales[:])
+            for n in range(PSUM_BANKS):
+                w1_pass(n, c)
+
+        for n in range(LAG):
             step(n)
-        quantise_u1(nc, psum, stage, identity[:], u1_rows, u1_codes[:], u1_scales[:])
-        for n in range(UNIT, BANKS + LAG):
+        quantise_u0_half(second_half)
+        for n in range(LAG, BANKS + LAG):
             step(n)

from contextlib import ExitStack

import concourse.mybir as mybir
from concourse.masks import make_identity

BF16 = mybir.dt.bfloat16
F32 = mybir.dt.float32
U32 = mybir.dt.uint32
U8 = mybir.dt.uint8
FP8X4 = mybir.dt.float8_e4m3fn_x4

P = 128
PACK = 4
K = P * PACK
R = 8
J = 1024
I = 512
J_BLOCKS = J // P
FACTOR_BLOCKS = 4
R_HALF = R // 2
UNIT = 4
STORE_BANKS = 2
STORES_IN_FLIGHT = 8
BANKS = R * J_BLOCKS
PSUM_BANKS = 8
LAG = PSUM_BANKS
SCALAR_SHARE = 8

FLOPS = 2 * K * (K * R) * J + 2 * K * (R * J) * I


def bank_indices(n):
    j_half, rest = divmod(n, BANKS // 2)
    r, place = divmod(rest, FACTOR_BLOCKS)
    return r, j_half * FACTOR_BLOCKS + place


def quantise_u0_blocks(nc, psum, stage, identity, rows, codes, scales):
    grouped = stage.tile([P, FACTOR_BLOCKS * P * PACK], BF16, align_bytes=64, name="u0_grouped")
    grouped_words = grouped[:].bitcast(F32).rearrange("x (b a u) -> x b a u", b=FACTOR_BLOCKS, u=2)
    for first in range(0, FACTOR_BLOCKS, 2):
        flipped = psum.tile([P, 2, 2, P], F32, name="u0_flipped", tag="one")
        for b in range(2):
            words = rows[:, first + b, :].bitcast(F32)
            for u in range(2):
                nc.tensor.transpose(flipped[:, b, u, :], words[:, u * P : (u + 1) * P], identity)
        source = flipped[:].rearrange("x b u a -> x b a u")
        if first == 0:
            nc.vector.tensor_copy(out=grouped_words[:, first : first + 2], in_=source)
        else:
            nc.scalar.copy(out=grouped_words[:, first : first + 2], in_=source)
    nc.vector.quantize_mx(out=codes.bitcast(FP8X4), scales=scales, in_=grouped[:])


def quantise_u1(nc, psum, stage, identity, rows, codes, scales):
    grouped = stage.tile([P, FACTOR_BLOCKS, P, PACK], BF16, align_bytes=64, name="u1_grouped")
    for b in range(FACTOR_BLOCKS):
        flipped = psum.tile([P, PACK, P], BF16, name="u1_flipped", tag="two")
        for t in range(PACK):
            nc.tensor.transpose(flipped[:, t, :], rows[:, b, t * P : (t + 1) * P], identity)
        source = flipped[:].rearrange("y t a -> y a t")
        if b % 2 == 0:
            nc.vector.tensor_copy(out=grouped[:, b], in_=source)
        else:
            nc.scalar.copy(out=grouped[:, b], in_=source)
    nc.vector.quantize_mx(
        out=codes.bitcast(FP8X4),
        scales=scales,
        in_=grouped[:].rearrange("y b a t -> y (b a t)"),
    )


def tile_mtl_net_tf_pa_kernel(tc, S, U0, U1, out):
    nc = tc.nc
    with ExitStack() as ctx:
        keep = ctx.enter_context(tc.tile_pool(name="keep", bufs=1))
        stage = ctx.enter_context(tc.tile_pool(name="stage", bufs=3))
        psum = ctx.enter_context(tc.psum_pool(name="psum", bufs=PSUM_BANKS // 2))

        u0_view = U0.rearrange("(a b) q -> a b q", b=J_BLOCKS)
        u0_rows = keep.tile([P, J_BLOCKS, K], BF16)
        first_half = slice(0, FACTOR_BLOCKS)
        second_half = slice(FACTOR_BLOCKS, J_BLOCKS)
        u1_rows = keep.tile([P, FACTOR_BLOCKS, K], BF16)
        s_view = S.rearrange("(u x e) p r -> x u e p r", u=2, e=2)
        s_raw = []
        for c in range(PACK):
            raw = keep.tile([P, PACK, P, R], BF16, name="s_raw%d" % c)
            for u in range(2):
                nc.sync.dma_start(
                    out=raw[:, 2 * u : 2 * u + 2, :, :], in_=s_view[:, u, :, c * P : (c + 1) * P, :]
                )
            s_raw.append(raw)
            if c == 0:
                nc.sync.dma_start(out=u0_rows[:, first_half, :], in_=u0_view[:, first_half, :])
                nc.sync.dma_start(out=u1_rows[:], in_=U1.rearrange("(b a) p -> a b p", a=P))
        nc.sync.dma_start(out=u0_rows[:, second_half, :], in_=u0_view[:, second_half, :])

        identity_words = keep.tile([P, P], F32)
        make_identity(nc, identity_words[:])
        identity = keep.tile([P, P], BF16)
        make_identity(nc, identity[:])

        u0_codes = keep.tile([P, J_BLOCKS, P], U32, align_bytes=64)
        u0_scales = keep.tile([P, J_BLOCKS, P], U8, align_bytes=64)
        u1_codes = keep.tile([P, I], U32, align_bytes=64)
        u1_scales = keep.tile([P, I], U8, align_bytes=64)
        s_codes = keep.tile([P, 2, PACK, R_HALF * P], U32, align_bytes=64)
        s_scales = keep.tile([P, 2, PACK, R_HALF * P], U8, align_bytes=64)
        s_grouped = {}
        w1_bank = {}
        w1_grouped = {}
        w1_codes = {}
        w1_scales = {}
        result = {}
        out_view = out.rearrange("r (a b) i -> r a b i", b=J_BLOCKS)

        def quantise_u0_half(blocks):
            quantise_u0_blocks(
                nc,
                psum,
                stage,
                identity_words[:],
                u0_rows[:, blocks, :],
                u0_codes[:, blocks, :].rearrange("x b a -> x (b a)"),
                u0_scales[:, blocks, :].rearrange("x b a -> x (b a)"),
            )

        def regroup_s(c):
            for half in range(2):
                s_grouped[half, c] = keep.tile(
                    [P, R_HALF, P, PACK], BF16, align_bytes=64, name="s_grouped%d%d" % (half, c)
                )
                target = s_grouped[half, c][:].rearrange("x r y t -> x y t r")
                source = s_raw[c][:, :, :, half * R_HALF : (half + 1) * R_HALF].rearrange(
                    "x t y r -> x y t r"
                )
                if half == 0:
                    nc.vector.tensor_copy(out=target, in_=source)
                else:
                    nc.scalar.copy(out=target, in_=source)

        def quantise_s(half, c):
            nc.vector.quantize_mx(
                out=s_codes[:, half, c, :].bitcast(FP8X4),
                scales=s_scales[:, half, c, :],
                in_=s_grouped[half, c][:].rearrange("x r y t -> x (r y t)"),
            )

        def w1_pass(n, c):
            r, b = bank_indices(n)
            half, r_low = divmod(r, R_HALF)
            if c == 0:
                early_second_tag = PSUM_BANKS // 2 <= n < PSUM_BANKS
                w1_bank[n] = psum.tile(
                    [P, PACK, P], F32, name="w1_bank", tag="two" if early_second_tag else "one"
                )
            nc.tensor.matmul_mx(
                out=w1_bank[n][:, c, :],
                lhsT=s_codes[:, half, c, r_low * P : (r_low + 1) * P].bitcast(FP8X4),
                lhsT_scale=s_scales[:, half, c, r_low * P : (r_low + 1) * P],
                rhs=u0_codes[:, b, :].bitcast(FP8X4),
                rhs_scale=u0_scales[:, b, :],
                start=True,
                stop=True,
            )

        def round_w1(n):
            unit, place = divmod(n, UNIT)
            if place == 0:
                w1_grouped[unit] = stage.tile(
                    [P, UNIT, P, PACK], BF16, align_bytes=64, name="w1_grouped"
                )
            source = w1_bank[n][:].rearrange("y c a -> y a c")
            if n % SCALAR_SHARE == SCALAR_SHARE - 1 or (n < LAG and n % UNIT != 0):
                nc.scalar.copy(out=w1_grouped[unit][:, place], in_=source)
            else:
                nc.vector.tensor_copy(out=w1_grouped[unit][:, place], in_=source)

        def quantise_w1(unit):
            w1_codes[unit] = stage.tile([P, UNIT * P], U32, align_bytes=64, name="w1_codes")
            w1_scales[unit] = stage.tile([P, UNIT * P], U8, align_bytes=64, name="w1_scales")
            nc.vector.quantize_mx(
                out=w1_codes[unit][:].bitcast(FP8X4),
                scales=w1_scales[unit][:],
                in_=w1_grouped[unit][:].rearrange("y u a c -> y (u a c)"),
            )

        def second_contraction(n):
            r, b = bank_indices(n)
            unit, place = divmod(n, UNIT)
            batch, slot = divmod(n, STORE_BANKS)
            if slot == 0:
                result[batch] = stage.tile(
                    [P, STORE_BANKS, I], F32, name="result", bufs=STORES_IN_FLIGHT
                )
            out_bank = psum.tile([P, I], F32, name="out_bank", tag="two")
            nc.tensor.matmul_mx(
                out=out_bank[:],
                lhsT=w1_codes[unit][:, place * P : (place + 1) * P].bitcast(FP8X4),
                lhsT_scale=w1_scales[unit][:, place * P : (place + 1) * P],
                rhs=u1_codes[:].bitcast(FP8X4),
                rhs_scale=u1_scales[:],
                start=True,
                stop=True,
            )
            if n >= BANKS - LAG and n % 2 == 1:
                nc.vector.tensor_copy(out=result[batch][:, slot, :], in_=out_bank[:])
            else:
                nc.scalar.copy(out=result[batch][:, slot, :], in_=out_bank[:])
            if slot == STORE_BANKS - 1:
                nc.sync.dma_start(out=out_view[r, :, b - slot : b + 1, :], in_=result[batch][:])

        def step(n):
            if PSUM_BANKS <= n < BANKS:
                for c in range(PACK):
                    w1_pass(n, c)
            if n < BANKS:
                round_w1(n)
            if n % UNIT == 0 and UNIT <= n <= BANKS:
                quantise_w1(n // UNIT - 1)
            if n % 2 == 1 and n // 2 < PACK:
                quantise_s(1, n // 2)
            if n >= LAG:
                second_contraction(n - LAG)

        for c in range(PACK):
            regroup_s(c)
            quantise_s(0, c)
            if c == 0:
                quantise_u0_half(first_half)
                quantise_u1(nc, psum, stage, identity[:], u1_rows, u1_codes[:], u1_scales[:])
            for n in range(PSUM_BANKS):
                w1_pass(n, c)

        for n in range(LAG):
            step(n)
        quantise_u0_half(second_half)
        for n in range(LAG, BANKS + LAG):
            step(n)
